import numpy as np
import ml_dtypes


def mxq(x, axis, fmt="e4m3"):
    dtype, down = {"e4m3": (ml_dtypes.float8_e4m3fn, 7), "e5m2": (ml_dtypes.float8_e5m2, 14)}[fmt]
    v = np.moveaxis(np.asarray(x, np.float32).astype(ml_dtypes.bfloat16).astype(np.float64), axis, -1)
    blocks = v.reshape(v.shape[:-1] + (-1, 32))
    amax = np.abs(blocks).max(-1, keepdims=True)
    byte = np.maximum(np.where(amax > 0, np.frexp(amax)[1] - 1 + 127, 0) - down, 1)
    scale = np.exp2(byte - 127.0)
    codes = (blocks / scale).astype(np.float32).astype(dtype).astype(np.float64)
    return np.moveaxis((codes * scale).reshape(v.shape), -1, axis)


WIDE = False


def mx_kscale(k):
    if not WIDE:
        return np.ones(k)
    levels = np.array([10, -10, 5, -5, 0])
    a = np.random.permutation(np.resize(levels, k // 512 * 4)).reshape(k // 512, 4)
    idx = np.arange(k)
    return np.exp2(a[idx // 512, idx % 128 // 32])


BF16 = ml_dtypes.bfloat16


def bf(x):
    return np.asarray(x, np.float32).astype(BF16)


def f64(x):
    return np.asarray(x).astype(np.float64)


H, S, QP, VP = 4, 512, 512, 512
HV = H * VP


def setup_inputs():
    s = mx_kscale(QP)
    return {
        "q": bf(np.random.standard_normal((H, S, QP)) * 1.5),
        "k": bf(np.random.standard_normal((H, S, QP)) * 1.5),
        "value": bf(np.random.standard_normal((S, QP)) * s[None, :]),
        "mask": bf(np.random.random((S, S))),
        "Wv": bf(np.random.standard_normal((H, VP, QP)) * 1.5 / np.sqrt(QP) / s[None, None, :]),
        "bv": bf(np.random.standard_normal((H, VP)) * 0.3),
    }


def reference(q, k, value, mask, Wv, bv):
    v = (mxq(f64(value), 1, "e4m3") @ mxq(f64(Wv), 2, "e4m3").transpose(0, 2, 1)) + f64(bv)[:, None, :]
    s = (f64(q) @ f64(k).transpose(0, 2, 1)) * f64(mask)[None, :, :] * (1.0 / np.sqrt(QP))
    e = np.exp(s - s.max(-1, keepdims=True))
    o = (mxq(e, 2, "e4m3") @ mxq(v, 1, "e4m3")) / e.sum(-1, keepdims=True)
    return o.transpose(1, 0, 2).reshape(S, HV)

@@ -1,0 +1,322 @@
+import math
+from contextlib import ExitStack
+
+import concourse.mybir as mybir
+from concourse.masks import make_identity
+
+BF16 = mybir.dt.bfloat16
+F32 = mybir.dt.float32
+U32 = mybir.dt.uint32
+U8 = mybir.dt.uint8
+FP8X4 = mybir.dt.float8_e4m3fn_x4
+ALU = mybir.AluOpType
+ACT = mybir.ActivationFunctionType
+AXIS = mybir.AxisListType
+
+P = 128
+H = 4
+S = 512
+D = 512
+V = 512
+T = S // P
+PACK = 4
+WORDS = D // 2
+PLANES = WORDS // P
+PAIR = 2 * P
+SCALE = 1.0 / math.sqrt(D)
+STEPS = H * T
+
+QK_AHEAD = 3
+WV_AHEAD = 4
+PROJECT_AHEAD = 3
+BIAS_AHEAD = 2
+EXP_BEHIND = 1
+OUT_BEHIND = 2
+
+FLOPS = 3 * H * 2 * S * D * V
+
+
+def transpose_words(nc, bank, rows, row_tiles, ident_f32):
+    words = rows[:].bitcast(F32)
+    n = len(row_tiles)
+    for u in range(PLANES):
+        for i in range(n):
+            first_word = row_tiles[i] * WORDS + u * P
+            nc.tensor.transpose(
+                bank[:, (u * n + i) * P : (u * n + i + 1) * P],
+                words[:, first_word : first_word + P],
+                ident_f32[:],
+            )
+
+
+def planes_side_by_side(bank):
+    return bank[:].rearrange("p (u r) -> p r u", u=PLANES)
+
+
+def as_words(grouped):
+    return grouped[:].bitcast(F32).rearrange("p (r u) -> p r u", u=PLANES)
+
+
+def tile_maskedmultiheadattention_pa_kernel(tc, q, k, value, mask, Wv, bv, out):
+    nc = tc.nc
+    with ExitStack() as ctx:
+        ctx.enter_context(tc.manual_schedule())
+        consts = ctx.enter_context(tc.tile_pool(name="consts", bufs=1))
+        per_head = ctx.enter_context(tc.tile_pool(name="per_head", bufs=H))
+        work = ctx.enter_context(tc.tile_pool(name="work", bufs=4))
+        ps_words = ctx.enter_context(tc.psum_pool(name="ps_words", bufs=3))
+        ps_scores = ctx.enter_context(tc.psum_pool(name="ps_scores", bufs=2))
+        ps_et = ctx.enter_context(tc.psum_pool(name="ps_et", bufs=1))
+        ps_mx = ctx.enter_context(tc.psum_pool(name="ps_mx", bufs=2))
+
+        bias_row = consts.tile([P, H * V], BF16)
+        nc.vector.memset(bias_row[:], 0.0)
+        nc.sync.dma_start(out=bias_row[0:1, :], in_=bv.rearrange("h v -> (h v)").unsqueeze(0))
+
+        def load_row_tiles(rows_sb, rows):
+            nc.sync.dma_start(
+                out=rows_sb[:].rearrange("p (t d) -> p t d", t=T),
+                in_=rows.rearrange("(t p) d -> p t d", p=P),
+            )
+
+        value_rows = consts.tile([P, T * D], BF16)
+        mask_sb = consts.tile([P, T, S], BF16)
+        k_rows, q_rows, wv_rows = [], [], []
+        for h in range(H):
+            k_sb = per_head.tile([P, T * D], BF16)
+            k_rows.append(k_sb)
+            q_sb = per_head.tile([P, T * D], BF16)
+            q_rows.append(q_sb)
+            wv_sb = per_head.tile([P, T * D], BF16)
+            wv_rows.append(wv_sb)
+        load_row_tiles(value_rows, value)
+        load_row_tiles(wv_rows[0], Wv[0])
+        for h in range(H):
+            load_row_tiles(k_rows[h], k[h])
+            if h > 0:
+                load_row_tiles(wv_rows[h], Wv[h])
+            nc.sync.dma_start(out=q_rows[h][:], in_=q[h].rearrange("(p t) d -> p (t d)", t=T))
+            if h == 0:
+                nc.sync.dma_start(out=mask_sb[:], in_=mask.rearrange("(p t) j -> p t j", t=T))
+        out_rows = out.rearrange("(p t) c -> p t c", t=T)
+
+        ident_f32 = consts.tile([P, P], F32)
+        make_identity(nc, ident_f32[:])
+        ident_bf16 = consts.tile([P, P], BF16)
+        make_identity(nc, ident_bf16[:])
+        ones = consts.tile([P, P], BF16)
+        nc.vector.memset(ones[:], 1.0)
+
+        table_warmer = consts.tile([P, 1], F32)
+        nc.scalar.activation(out=table_warmer[:], in_=ones[:, 0:1], func=ACT.Exp)
+
+        bias = consts.tile([P, H * V], F32)
+        for h in range(H):
+            bias_ps = ps_mx.tile([P, V], F32, name="mx_bank")
+            nc.tensor.matmul(
+                out=bias_ps[:], lhsT=ones[:], rhs=bias_row[:, h * V : (h + 1) * V], start=True, stop=True
+            )
+            nc.vector.tensor_copy(out=bias[:, h * V : (h + 1) * V], in_=bias_ps[:])
+
+        value_grouped = consts.tile([P, S * PACK], BF16, align_bytes=64)
+        value_codes = consts.tile([P, S], U32, align_bytes=64)
+        value_scales = consts.tile([P, S], U8, align_bytes=64)
+        for pair in range(T // 2):
+            bank = ps_words.tile([P, PLANES * PAIR], F32, name="word_bank")
+            transpose_words(nc, bank, value_rows, [2 * pair, 2 * pair + 1], ident_f32)
+            nc.scalar.copy(
+                out=as_words(value_grouped)[:, pair * PAIR : (pair + 1) * PAIR, :],
+                in_=planes_side_by_side(bank),
+            )
+        nc.vector.quantize_mx(
+            out=value_codes[:].bitcast(FP8X4), scales=value_scales[:], in_=value_grouped[:]
+        )
+
+        tiles = {}
+
+        def transpose_wv(m):
+            if not 0 <= m < STEPS:
+                return
+            h, c = divmod(m, T)
+            bank = ps_words.tile([P, PLANES * P], F32, name="word_bank")
+            transpose_words(nc, bank, wv_rows[h], [c], ident_f32)
+            grouped = work.tile([P, P * PACK], BF16, name="wv_grouped", align_bytes=64)
+            nc.scalar.copy(out=as_words(grouped), in_=planes_side_by_side(bank))
+            tiles["wv_grouped", m] = grouped
+
+        def quantise_wv(m):
+            if not 0 <= m < STEPS:
+                return
+            codes = work.tile([P, P], U32, name="wv_codes", align_bytes=64)
+            scales = work.tile([P, P], U8, name="wv_scales", align_bytes=64)
+            nc.vector.quantize_mx(
+                out=codes[:].bitcast(FP8X4), scales=scales[:], in_=tiles["wv_grouped", m][:]
+            )
+            tiles["wv_codes", m] = codes
+            tiles["wv_scales", m] = scales
+
+        def project_v(m):
+            if not 0 <= m < STEPS:
+                return
+            v_ps = ps_mx.tile([P, T, P], F32, name="mx_bank")
+            for t in range(T):
+                keys = slice(t * P, (t + 1) * P)
+                nc.tensor.matmul_mx(
+                    out=v_ps[:, t, :],
+                    lhsT=value_codes[:, keys].bitcast(FP8X4),
+                    lhsT_scale=value_scales[:, keys],
+                    rhs=tiles["wv_codes", m][:].bitcast(FP8X4),
+                    rhs_scale=tiles["wv_scales", m][:],
+                    start=True,
+                    stop=True,
+                )
+            tiles["v_ps", m] = v_ps
+
+        def add_bias(m):
+            if not 0 <= m < STEPS:
+                return
+            h, c = divmod(m, T)
+            if c == 0:
+                tiles["v_grouped", h] = per_head.tile([P, V, PACK], BF16, name="v_grouped", align_bytes=64)
+                tiles["v_codes", h] = per_head.tile([P, V], U32, name="v_codes", align_bytes=64)
+                tiles["v_scales", h] = per_head.tile([P, V], U8, name="v_scales", align_bytes=64)
+            cols = slice(c * P, (c + 1) * P)
+            grouped = tiles["v_grouped", h][:, cols, :]
+            nc.vector.tensor_tensor(
+                out=grouped,
+                in0=tiles["v_ps", m][:].rearrange("p t c -> p c t"),
+                in1=bias[:, m * P : (m + 1) * P].unsqueeze(2).to_broadcast([P, P, T]),
+                op=ALU.add,
+            )
+            nc.vector.quantize_mx(
+                out=tiles["v_codes", h][:, cols].bitcast(FP8X4),
+                scales=tiles["v_scales", h][:, cols],
+                in_=grouped.rearrange("p c t -> p (c t)"),
+            )
+
+        def transpose_qk(m):
+            if not 0 <= m < STEPS:
+                return
+            h, quarter = divmod(m, T)
+            name = "k_t" if quarter < 2 else "q_t"
+            rows = k_rows[h] if quarter < 2 else q_rows[h]
+            pair = quarter % 2
+            if pair == 0:
+                tiles[name, h] = per_head.tile([P, PLANES, S, 2], BF16, name=name)
+            bank = ps_words.tile([P, PLANES * PAIR], F32, name="word_bank")
+            transpose_words(nc, bank, rows, [2 * pair, 2 * pair + 1], ident_f32)
+            nc.scalar.copy(
+                out=tiles[name, h][:, :, pair * PAIR : (pair + 1) * PAIR, :].rearrange("p u r e -> p u (r e)"),
+                in_=bank[:].bitcast(BF16).rearrange("p (u x) -> p u x", u=PLANES),
+            )
+
+        def scores(n):
+            if not 0 <= n < STEPS:
+                return
+            h, t = divmod(n, T)
+            s_ps = ps_scores.tile([P, S], F32, name="s_ps")
+            for u in range(PLANES):
+                for e in range(2):
+                    nc.tensor.matmul(
+                        out=s_ps[:],
+                        lhsT=tiles["q_t", h][:, u, t * P : (t + 1) * P, e],
+                        rhs=tiles["k_t", h][:, u, :, e],
+                        start=(u == 0 and e == 0),
+                        stop=(u == PLANES - 1 and e == 1),
+                    )
+            tiles["s_ps", n] = s_ps
+
+        def mask_and_max(n):
+            if not 0 <= n < STEPS:
+                return
+            masked = work.tile([P, S], F32, name="masked")
+            nc.vector.scalar_tensor_tensor(
+                out=masked[:],
+                in0=tiles["s_ps", n][:],
+                scalar=SCALE,
+                in1=mask_sb[:, n % T, :],
+                op0=ALU.mult,
+                op1=ALU.mult,
+            )
+            neg_max = work.tile([P, 1], F32, name="neg_max")
+            nc.vector.tensor_reduce(out=neg_max[:], in_=masked[:], axis=AXIS.X, op=ALU.max, negate=True)
+            tiles["masked", n] = masked
+            tiles["neg_max", n] = neg_max
+
+        def exponential(n):
+            if not 0 <= n < STEPS:
+                return
+            e_sb = work.tile([P, S], BF16, name="e_sb")
+            row_sum = work.tile([P, 1], F32, name="row_sum")
+            nc.scalar.activation(
+                out=e_sb[:],
+                in_=tiles["masked", n][:],
+                func=ACT.Exp,
+                bias=tiles["neg_max", n][:],
+                scale=1.0,
+                accum_out=row_sum[:],
+            )
+            tiles["e_sb", n] = e_sb
+            tiles["row_sum", n] = row_sum
+
+        def reciprocal(n):
+            if not 0 <= n < STEPS:
+                return
+            inv_sum = work.tile([P, 1], F32, name="inv_sum")
+            nc.vector.reciprocal(out=inv_sum[:], in_=tiles["row_sum", n][:])
+            tiles["inv_sum", n] = inv_sum
+
+        def transpose_e(n):
+            if not 0 <= n < STEPS:
+                return
+            et_ps = ps_et.tile([P, T, P], BF16, name="et_ps")
+            for t in range(T):
+                nc.tensor.transpose(et_ps[:, t, :], tiles["e_sb", n][:, t * P : (t + 1) * P], ident_bf16[:])
+            e_grouped = work.tile([P, P, PACK], BF16, name="e_grouped", align_bytes=64)
+            nc.scalar.copy(out=e_grouped[:], in_=et_ps[:].rearrange("p t r -> p r t"))
+            tiles["e_grouped", n] = e_grouped
+
+        def quantise_e(n):
+            if not 0 <= n < STEPS:
+                return
+            codes = work.tile([P, P], U32, name="e_codes", align_bytes=64)
+            scales = work.tile([P, P], U8, name="e_scales", align_bytes=64)
+            nc.vector.quantize_mx(
+                out=codes[:].bitcast(FP8X4),
+                scales=scales[:],
+                in_=tiles["e_grouped", n][:].rearrange("p r t -> p (r t)"),
+            )
+            tiles["e_codes", n] = codes
+            tiles["e_scales", n] = scales
+
+        def output(n):
+            if not 0 <= n < STEPS:
+                return
+            h, t = divmod(n, T)
+            o_ps = ps_mx.tile([P, V], F32, name="mx_bank")
+            nc.tensor.matmul_mx(
+                out=o_ps[:],
+                lhsT=tiles["e_codes", n][:].bitcast(FP8X4),
+                lhsT_scale=tiles["e_scales", n][:],
+                rhs=tiles["v_codes", h][:].bitcast(FP8X4),
+                rhs_scale=tiles["v_scales", h][:],
+                start=True,
+                stop=True,
+            )
+            o_sb = work.tile([P, V], F32, name="o_sb")
+            nc.scalar.activation(out=o_sb[:], in_=o_ps[:], func=ACT.Copy, scale=tiles["inv_sum", n][:])
+            nc.sync.dma_start(out=out_rows[:, t, h * V : (h + 1) * V], in_=o_sb[:])
+
+        for step in range(-WV_AHEAD, STEPS + OUT_BEHIND):
+            exponential(step - EXP_BEHIND)
+            scores(step)
+            transpose_wv(step + WV_AHEAD)
+            transpose_qk(step + QK_AHEAD)
+            transpose_e(step - EXP_BEHIND)
+            quantise_e(step - OUT_BEHIND)
+            quantise_wv(step + PROJECT_AHEAD)
+            add_bias(step + BIAS_AHEAD)
+            output(step - OUT_BEHIND)
+            project_v(step + PROJECT_AHEAD)
+            mask_and_max(step)
+            reciprocal(step - EXP_BEHIND)

@@ -31,7 +31,8 @@ WV_AHEAD = 4
 PROJECT_AHEAD = 3
 BIAS_AHEAD = 2
 EXP_BEHIND = 1
-OUT_BEHIND = 2
+EV_BEHIND = 2
+OUT_BEHIND = 3
 
 FLOPS = 3 * H * 2 * S * D * V
 
@@ -180,18 +181,22 @@ def tile_maskedmultiheadattention_pa_kernel(tc, q, k, value, mask, Wv, bv, out):
                 tiles["v_grouped", h] = per_head.tile([P, V, PACK], BF16, name="v_grouped", align_bytes=64)
                 tiles["v_codes", h] = per_head.tile([P, V], U32, name="v_codes", align_bytes=64)
                 tiles["v_scales", h] = per_head.tile([P, V], U8, name="v_scales", align_bytes=64)
-            cols = slice(c * P, (c + 1) * P)
-            grouped = tiles["v_grouped", h][:, cols, :]
             nc.vector.tensor_tensor(
-                out=grouped,
+                out=tiles["v_grouped", h][:, c * P : (c + 1) * P, :],
                 in0=tiles["v_ps", m][:].rearrange("p t c -> p c t"),
                 in1=bias[:, m * P : (m + 1) * P].unsqueeze(2).to_broadcast([P, P, T]),
                 op=ALU.add,
             )
+
+        def quantise_v(m):
+            if not 0 <= m < STEPS:
+                return
+            h, c = divmod(m, T)
+            cols = slice(c * P, (c + 1) * P)
             nc.vector.quantize_mx(
                 out=tiles["v_codes", h][:, cols].bitcast(FP8X4),
                 scales=tiles["v_scales", h][:, cols],
-                in_=grouped.rearrange("p c t -> p (c t)"),
+                in_=tiles["v_grouped", h][:, cols, :].rearrange("p c t -> p (c t)"),
             )
 
         def transpose_qk(m):
@@ -226,7 +231,7 @@ def tile_maskedmultiheadattention_pa_kernel(tc, q, k, value, mask, Wv, bv, out):
                     )
             tiles["s_ps", n] = s_ps
 
-        def mask_and_max(n):
+        def apply_mask(n):
             if not 0 <= n < STEPS:
                 return
             masked = work.tile([P, S], F32, name="masked")
@@ -238,9 +243,15 @@ def tile_maskedmultiheadattention_pa_kernel(tc, q, k, value, mask, Wv, bv, out):
                 op0=ALU.mult,
                 op1=ALU.mult,
             )
-            neg_max = work.tile([P, 1], F32, name="neg_max")
-            nc.vector.tensor_reduce(out=neg_max[:], in_=masked[:], axis=AXIS.X, op=ALU.max, negate=True)
             tiles["masked", n] = masked
+
+        def row_max(n):
+            if not 0 <= n < STEPS:
+                return
+            neg_max = work.tile([P, 1], F32, name="neg_max")
+            nc.vector.tensor_reduce(
+                out=neg_max[:], in_=tiles["masked", n][:], axis=AXIS.X, op=ALU.max, negate=True
+            )
             tiles["neg_max", n] = neg_max
 
         def exponential(n):
@@ -289,10 +300,10 @@ def tile_maskedmultiheadattention_pa_kernel(tc, q, k, value, mask, Wv, bv, out):
             tiles["e_codes", n] = codes
             tiles["e_scales", n] = scales
 
-        def output(n):
+        def multiply_e_v(n):
             if not 0 <= n < STEPS:
                 return
-            h, t = divmod(n, T)
+            h = n // T
             o_ps = ps_mx.tile([P, V], F32, name="mx_bank")
             nc.tensor.matmul_mx(
                 out=o_ps[:],
@@ -303,20 +314,31 @@ def tile_maskedmultiheadattention_pa_kernel(tc, q, k, value, mask, Wv, bv, out):
                 start=True,
                 stop=True,
             )
+            tiles["o_ps", n] = o_ps
+
+        def divide_and_store(n):
+            if not 0 <= n < STEPS:
+                return
+            h, t = divmod(n, T)
             o_sb = work.tile([P, V], F32, name="o_sb")
-            nc.scalar.activation(out=o_sb[:], in_=o_ps[:], func=ACT.Copy, scale=tiles["inv_sum", n][:])
+            nc.scalar.activation(
+                out=o_sb[:], in_=tiles["o_ps", n][:], func=ACT.Copy, scale=tiles["inv_sum", n][:]
+            )
             nc.sync.dma_start(out=out_rows[:, t, h * V : (h + 1) * V], in_=o_sb[:])
 
         for step in range(-WV_AHEAD, STEPS + OUT_BEHIND):
             exponential(step - EXP_BEHIND)
+            divide_and_store(step - OUT_BEHIND)
             scores(step)
             transpose_wv(step + WV_AHEAD)
             transpose_qk(step + QK_AHEAD)
             transpose_e(step - EXP_BEHIND)
-            quantise_e(step - OUT_BEHIND)
+            quantise_e(step - EV_BEHIND)
             quantise_wv(step + PROJECT_AHEAD)
             add_bias(step + BIAS_AHEAD)
-            output(step - OUT_BEHIND)
+            multiply_e_v(step - EV_BEHIND)
             project_v(step + PROJECT_AHEAD)
-            mask_and_max(step)
+            apply_mask(step)
+            quantise_v(step + BIAS_AHEAD)
             reciprocal(step - EXP_BEHIND)
+            row_max(step)

@@ -6,6 +6,7 @@ from concourse.masks import make_identity
 
 BF16 = mybir.dt.bfloat16
 F32 = mybir.dt.float32
+I32 = mybir.dt.int32
 U32 = mybir.dt.uint32
 U8 = mybir.dt.uint8
 FP8X4 = mybir.dt.float8_e4m3fn_x4
@@ -71,8 +72,7 @@ def tile_maskedmultiheadattention_pa_kernel(tc, q, k, value, mask, Wv, bv, out):
         ps_mx = ctx.enter_context(tc.psum_pool(name="ps_mx", bufs=2))
 
         bias_row = consts.tile([P, H * V], BF16)
-        nc.vector.memset(bias_row[:], 0.0)
-        nc.sync.dma_start(out=bias_row[0:1, :], in_=bv.rearrange("h v -> (h v)").unsqueeze(0))
+        nc.vector.memset(bias_row[:].bitcast(I32), 0)
 
         def load_row_tiles(rows_sb, rows):
             nc.sync.dma_start(
@@ -90,7 +90,11 @@ def tile_maskedmultiheadattention_pa_kernel(tc, q, k, value, mask, Wv, bv, out):
             q_rows.append(q_sb)
             wv_sb = per_head.tile([P, T * D], BF16)
             wv_rows.append(wv_sb)
-        load_row_tiles(value_rows, value)
+        nc.sync.dma_start(
+            out=value_rows[:].rearrange("p (u x) -> p u x", u=PLANES),
+            in_=value.rearrange("(u p e) d -> p u (e d)", u=PLANES, e=2),
+        )
+        nc.sync.dma_start(out=bias_row[0:1, :], in_=bv.rearrange("h v -> (h v)").unsqueeze(0))
         load_row_tiles(wv_rows[0], Wv[0])
         for h in range(H):
             load_row_tiles(k_rows[h], k[h])
@@ -103,21 +107,11 @@ def tile_maskedmultiheadattention_pa_kernel(tc, q, k, value, mask, Wv, bv, out):
 
         ident_f32 = consts.tile([P, P], F32)
         make_identity(nc, ident_f32[:])
-        ident_bf16 = consts.tile([P, P], BF16)
-        make_identity(nc, ident_bf16[:])
         ones = consts.tile([P, P], BF16)
         nc.vector.memset(ones[:], 1.0)
 
         table_warmer = consts.tile([P, 1], F32)
         nc.scalar.activation(out=table_warmer[:], in_=ones[:, 0:1], func=ACT.Exp)
-
-        bias = consts.tile([P, H * V], F32)
-        for h in range(H):
-            bias_ps = ps_mx.tile([P, V], F32, name="mx_bank")
-            nc.tensor.matmul(
-                out=bias_ps[:], lhsT=ones[:], rhs=bias_row[:, h * V : (h + 1) * V], start=True, stop=True
-            )
-            nc.vector.tensor_copy(out=bias[:, h * V : (h + 1) * V], in_=bias_ps[:])
 
         value_grouped = consts.tile([P, S * PACK], BF16, align_bytes=64)
         value_codes = consts.tile([P, S], U32, align_bytes=64)
@@ -132,6 +126,17 @@ def tile_maskedmultiheadattention_pa_kernel(tc, q, k, value, mask, Wv, bv, out):
         nc.vector.quantize_mx(
             out=value_codes[:].bitcast(FP8X4), scales=value_scales[:], in_=value_grouped[:]
         )
+
+        bias = consts.tile([P, H * V], F32)
+        for h in range(H):
+            bias_ps = ps_mx.tile([P, V], F32, name="mx_bank")
+            nc.tensor.matmul(
+                out=bias_ps[:], lhsT=ones[:], rhs=bias_row[:, h * V : (h + 1) * V], start=True, stop=True
+            )
+            if h % 2 == 0:
+                nc.vector.tensor_copy(out=bias[:, h * V : (h + 1) * V], in_=bias_ps[:])
+            else:
+                nc.scalar.copy(out=bias[:, h * V : (h + 1) * V], in_=bias_ps[:])
 
         tiles = {}
 
@@ -280,11 +285,10 @@ def tile_maskedmultiheadattention_pa_kernel(tc, q, k, value, mask, Wv, bv, out):
         def transpose_e(n):
             if not 0 <= n < STEPS:
                 return
-            et_ps = ps_et.tile([P, T, P], BF16, name="et_ps")
-            for t in range(T):
-                nc.tensor.transpose(et_ps[:, t, :], tiles["e_sb", n][:, t * P : (t + 1) * P], ident_bf16[:])
-            e_grouped = work.tile([P, P, PACK], BF16, name="e_grouped", align_bytes=64)
-            nc.scalar.copy(out=e_grouped[:], in_=et_ps[:].rearrange("p t r -> p r t"))
+            et_ps = ps_et.tile([P, PLANES * P], F32, name="et_ps")
+            transpose_words(nc, et_ps, tiles["e_sb", n], [0], ident_f32)
+            e_grouped = work.tile([P, P * PACK], BF16, name="e_grouped", align_bytes=64)
+            nc.scalar.copy(out=as_words(e_grouped), in_=planes_side_by_side(et_ps))
             tiles["e_grouped", n] = e_grouped
 
         def quantise_e(n):
@@ -295,7 +299,7 @@ def tile_maskedmultiheadattention_pa_kernel(tc, q, k, value, mask, Wv, bv, out):
             nc.vector.quantize_mx(
                 out=codes[:].bitcast(FP8X4),
                 scales=scales[:],
-                in_=tiles["e_grouped", n][:].rearrange("p r t -> p (r t)"),
+                in_=tiles["e_grouped", n][:],
             )
             tiles["e_codes", n] = codes
             tiles["e_scales", n] = scales

@@ -27,13 +27,18 @@ PAIR = 2 * P
 SCALE = 1.0 / math.sqrt(D)
 STEPS = H * T
 
-QK_AHEAD = 3
-WV_AHEAD = 4
-PROJECT_AHEAD = 3
-BIAS_AHEAD = 2
-EXP_BEHIND = 1
-EV_BEHIND = 2
-OUT_BEHIND = 3
+QK = 4
+SCORES = 1
+WV_TRANSPOSE = 1
+WV_QUANTISE = 0
+PROJECT = -1
+BIAS = -2
+V_QUANTISE = -3
+EXP = -1
+E_TRANSPOSE = -2
+E_QUANTISE = -6
+EV = -7
+OUT = -7
 
 FLOPS = 3 * H * 2 * S * D * V
 
@@ -65,11 +70,11 @@ def tile_maskedmultiheadattention_pa_kernel(tc, q, k, value, mask, Wv, bv, out):
         ctx.enter_context(tc.manual_schedule())
         consts = ctx.enter_context(tc.tile_pool(name="consts", bufs=1))
         per_head = ctx.enter_context(tc.tile_pool(name="per_head", bufs=H))
-        work = ctx.enter_context(tc.tile_pool(name="work", bufs=4))
-        ps_words = ctx.enter_context(tc.psum_pool(name="ps_words", bufs=3))
+        work = ctx.enter_context(tc.tile_pool(name="work", bufs=8))
+        ps_words = ctx.enter_context(tc.psum_pool(name="ps_words", bufs=2))
         ps_scores = ctx.enter_context(tc.psum_pool(name="ps_scores", bufs=2))
         ps_et = ctx.enter_context(tc.psum_pool(name="ps_et", bufs=1))
-        ps_mx = ctx.enter_context(tc.psum_pool(name="ps_mx", bufs=2))
+        ps_mx = ctx.enter_context(tc.psum_pool(name="ps_mx", bufs=3))
 
         bias_row = consts.tile([P, H * V], BF16)
         nc.vector.memset(bias_row[:].bitcast(I32), 0)
@@ -90,19 +95,34 @@ def tile_maskedmultiheadattention_pa_kernel(tc, q, k, value, mask, Wv, bv, out):
             q_rows.append(q_sb)
             wv_sb = per_head.tile([P, T * D], BF16)
             wv_rows.append(wv_sb)
+        def load_row_pair(rows_sb, rows, pair):
+            tiles_of_pair = slice(2 * pair, 2 * pair + 2)
+            nc.sync.dma_start(
+                out=rows_sb[:].rearrange("p (t d) -> p t d", t=T)[:, tiles_of_pair, :],
+                in_=rows.rearrange("(t p) d -> p t d", p=P)[:, tiles_of_pair, :],
+            )
+
+        def load_queries(h, first=0, last=T):
+            cols = slice(first * D, last * D)
+            nc.sync.dma_start(
+                out=q_rows[h][:, cols], in_=q[h].rearrange("(p t) d -> p (t d)", t=T)[:, cols]
+            )
+
+        load_row_pair(k_rows[0], k[0], 0)
+        load_row_pair(k_rows[0], k[0], 1)
+        nc.sync.dma_start(out=bias_row[0:1, :], in_=bv.rearrange("h v -> (h v)").unsqueeze(0))
+        load_queries(0, 0, T // 2)
+        load_queries(0, T // 2, T)
+        nc.sync.dma_start(out=mask_sb[:], in_=mask.rearrange("(p t) j -> p t j", t=T))
         nc.sync.dma_start(
             out=value_rows[:].rearrange("p (u x) -> p u x", u=PLANES),
             in_=value.rearrange("(u p e) d -> p u (e d)", u=PLANES, e=2),
         )
-        nc.sync.dma_start(out=bias_row[0:1, :], in_=bv.rearrange("h v -> (h v)").unsqueeze(0))
         load_row_tiles(wv_rows[0], Wv[0])
-        for h in range(H):
+        for h in range(1, H):
             load_row_tiles(k_rows[h], k[h])
-            if h > 0:
-                load_row_tiles(wv_rows[h], Wv[h])
-            nc.sync.dma_start(out=q_rows[h][:], in_=q[h].rearrange("(p t) d -> p (t d)", t=T))
-            if h == 0:
-                nc.sync.dma_start(out=mask_sb[:], in_=mask.rearrange("(p t) j -> p t j", t=T))
+            load_queries(h)
+            load_row_tiles(wv_rows[h], Wv[h])
         out_rows = out.rearrange("(p t) c -> p t c", t=T)
 
         ident_f32 = consts.tile([P, P], F32)
@@ -116,27 +136,34 @@ def tile_maskedmultiheadattention_pa_kernel(tc, q, k, value, mask, Wv, bv, out):
         value_grouped = consts.tile([P, S * PACK], BF16, align_bytes=64)
         value_codes = consts.tile([P, S], U32, align_bytes=64)
         value_scales = consts.tile([P, S], U8, align_bytes=64)
-        for pair in range(T // 2):
+
+        def transpose_value(pair):
             bank = ps_words.tile([P, PLANES * PAIR], F32, name="word_bank")
             transpose_words(nc, bank, value_rows, [2 * pair, 2 * pair + 1], ident_f32)
             nc.scalar.copy(
                 out=as_words(value_grouped)[:, pair * PAIR : (pair + 1) * PAIR, :],
                 in_=planes_side_by_side(bank),
             )
-        nc.vector.quantize_mx(
-            out=value_codes[:].bitcast(FP8X4), scales=value_scales[:], in_=value_grouped[:]
-        )
 
-        bias = consts.tile([P, H * V], F32)
-        for h in range(H):
-            bias_ps = ps_mx.tile([P, V], F32, name="mx_bank")
-            nc.tensor.matmul(
-                out=bias_ps[:], lhsT=ones[:], rhs=bias_row[:, h * V : (h + 1) * V], start=True, stop=True
+        def quantise_value():
+            nc.vector.quantize_mx(
+                out=value_codes[:].bitcast(FP8X4), scales=value_scales[:], in_=value_grouped[:]
             )
-            if h % 2 == 0:
-                nc.vector.tensor_copy(out=bias[:, h * V : (h + 1) * V], in_=bias_ps[:])
-            else:
-                nc.scalar.copy(out=bias[:, h * V : (h + 1) * V], in_=bias_ps[:])
+
+        bias = consts.tile([P, H * V], BF16)
+
+        def spread_bias(pair):
+            bias_ps = ps_mx.tile([P, 2 * V], BF16, name="mx_bank")
+            for i in range(2):
+                h = 2 * pair + i
+                nc.tensor.matmul(
+                    out=bias_ps[:, i * V : (i + 1) * V],
+                    lhsT=ones[:],
+                    rhs=bias_row[:, h * V : (h + 1) * V],
+                    start=True,
+                    stop=True,
+                )
+            nc.vector.tensor_copy(out=bias[:, 2 * pair * V : 2 * (pair + 1) * V], in_=bias_ps[:])
 
         tiles = {}
 
@@ -215,9 +242,12 @@ def tile_maskedmultiheadattention_pa_kernel(tc, q, k, value, mask, Wv, bv, out):
                 tiles[name, h] = per_head.tile([P, PLANES, S, 2], BF16, name=name)
             bank = ps_words.tile([P, PLANES * PAIR], F32, name="word_bank")
             transpose_words(nc, bank, rows, [2 * pair, 2 * pair + 1], ident_f32)
-            nc.scalar.copy(
-                out=tiles[name, h][:, :, pair * PAIR : (pair + 1) * PAIR, :].rearrange("p u r e -> p u (r e)"),
-                in_=bank[:].bitcast(BF16).rearrange("p (u x) -> p u x", u=PLANES),
+            copy = nc.vector.tensor_copy if h == 0 and pair == 0 else nc.scalar.copy
+            copy(
+                out=tiles[name, h][:, :, pair * PAIR : (pair + 1) * PAIR, :]
+                .rearrange("p u r e -> p u (r e)")
+                .bitcast(F32),
+                in_=bank[:].rearrange("p (u r) -> p u r", u=PLANES),
             )
 
         def scores(n):
@@ -330,19 +360,29 @@ def tile_maskedmultiheadattention_pa_kernel(tc, q, k, value, mask, Wv, bv, out):
             )
             nc.sync.dma_start(out=out_rows[:, t, h * V : (h + 1) * V], in_=o_sb[:])
 
-        for step in range(-WV_AHEAD, STEPS + OUT_BEHIND):
-            exponential(step - EXP_BEHIND)
-            divide_and_store(step - OUT_BEHIND)
-            scores(step)
-            transpose_wv(step + WV_AHEAD)
-            transpose_qk(step + QK_AHEAD)
-            transpose_e(step - EXP_BEHIND)
-            quantise_e(step - EV_BEHIND)
-            quantise_wv(step + PROJECT_AHEAD)
-            add_bias(step + BIAS_AHEAD)
-            multiply_e_v(step - EV_BEHIND)
-            project_v(step + PROJECT_AHEAD)
+        for step in range(-QK, STEPS - OUT):
+            exponential(step + EXP)
+            if step == -1:
+                spread_bias(1)
+            quantise_e(step + E_QUANTISE)
+            quantise_v(step + V_QUANTISE)
             apply_mask(step)
-            quantise_v(step + BIAS_AHEAD)
-            reciprocal(step - EXP_BEHIND)
+            if step == -1:
+                transpose_value(0)
+            multiply_e_v(step + EV)
+            if step == 0:
+                quantise_value()
+            if step == -3:
+                spread_bias(0)
+            divide_and_store(step + OUT)
+            if step == -1:
+                transpose_value(1)
+            scores(step + SCORES)
+            add_bias(step + BIAS)
+            transpose_qk(step + QK)
+            reciprocal(step + E_QUANTISE)
+            transpose_wv(step + WV_TRANSPOSE)
+            transpose_e(step + E_TRANSPOSE)
+            project_v(step + PROJECT)
             row_max(step)
+            quantise_wv(step + WV_QUANTISE)

@@ -79,11 +79,9 @@ def tile_maskedmultiheadattention_pa_kernel(tc, q, k, value, mask, Wv, bv, out):
         bias_row = consts.tile([P, H * V], BF16)
         nc.vector.memset(bias_row[:].bitcast(I32), 0)
 
-        def load_row_tiles(rows_sb, rows):
-            nc.sync.dma_start(
-                out=rows_sb[:].rearrange("p (t d) -> p t d", t=T),
-                in_=rows.rearrange("(t p) d -> p t d", p=P),
-            )
+        def load_rows(rows_sb, rows, first=0, last=T):
+            cols = slice(first * D, last * D)
+            nc.sync.dma_start(out=rows_sb[:, cols], in_=rows.rearrange("(p t) d -> p (t d)", t=T)[:, cols])
 
         value_rows = consts.tile([P, T * D], BF16)
         mask_sb = consts.tile([P, T, S], BF16)
@@ -95,34 +93,21 @@ def tile_maskedmultiheadattention_pa_kernel(tc, q, k, value, mask, Wv, bv, out):
             q_rows.append(q_sb)
             wv_sb = per_head.tile([P, T * D], BF16)
             wv_rows.append(wv_sb)
-        def load_row_pair(rows_sb, rows, pair):
-            tiles_of_pair = slice(2 * pair, 2 * pair + 2)
-            nc.sync.dma_start(
-                out=rows_sb[:].rearrange("p (t d) -> p t d", t=T)[:, tiles_of_pair, :],
-                in_=rows.rearrange("(t p) d -> p t d", p=P)[:, tiles_of_pair, :],
-            )
-
-        def load_queries(h, first=0, last=T):
-            cols = slice(first * D, last * D)
-            nc.sync.dma_start(
-                out=q_rows[h][:, cols], in_=q[h].rearrange("(p t) d -> p (t d)", t=T)[:, cols]
-            )
-
-        load_row_pair(k_rows[0], k[0], 0)
-        load_row_pair(k_rows[0], k[0], 1)
+        load_rows(k_rows[0], k[0], 0, T // 2)
+        load_rows(k_rows[0], k[0], T // 2, T)
         nc.sync.dma_start(out=bias_row[0:1, :], in_=bv.rearrange("h v -> (h v)").unsqueeze(0))
-        load_queries(0, 0, T // 2)
-        load_queries(0, T // 2, T)
+        load_rows(q_rows[0], q[0], 0, T // 2)
+        load_rows(q_rows[0], q[0], T // 2, T)
         nc.sync.dma_start(out=mask_sb[:], in_=mask.rearrange("(p t) j -> p t j", t=T))
         nc.sync.dma_start(
             out=value_rows[:].rearrange("p (u x) -> p u x", u=PLANES),
             in_=value.rearrange("(u p e) d -> p u (e d)", u=PLANES, e=2),
         )
-        load_row_tiles(wv_rows[0], Wv[0])
+        load_rows(wv_rows[0], Wv[0])
         for h in range(1, H):
-            load_row_tiles(k_rows[h], k[h])
-            load_queries(h)
-            load_row_tiles(wv_rows[h], Wv[h])
+            load_rows(k_rows[h], k[h])
+            load_rows(q_rows[h], q[h])
+            load_rows(wv_rows[h], Wv[h])
         out_rows = out.rearrange("(p t) c -> p t c", t=T)
 
         ident_f32 = consts.tile([P, P], F32)
@@ -216,7 +201,10 @@ def tile_maskedmultiheadattention_pa_kernel(tc, q, k, value, mask, Wv, bv, out):
             nc.vector.tensor_tensor(
                 out=tiles["v_grouped", h][:, c * P : (c + 1) * P, :],
                 in0=tiles["v_ps", m][:].rearrange("p t c -> p c t"),
-                in1=bias[:, m * P : (m + 1) * P].unsqueeze(2).to_broadcast([P, P, T]),
+                in1=bias[:, h * V : (h + 1) * V]
+                .rearrange("p (r c) -> p r c", c=T)[:, :, c]
+                .unsqueeze(2)
+                .to_broadcast([P, P, T]),
                 op=ALU.add,
             )
 
@@ -235,20 +223,35 @@ def tile_maskedmultiheadattention_pa_kernel(tc, q, k, value, mask, Wv, bv, out):
             if not 0 <= m < STEPS:
                 return
             h, quarter = divmod(m, T)
-            name = "k_t" if quarter < 2 else "q_t"
-            rows = k_rows[h] if quarter < 2 else q_rows[h]
-            pair = quarter % 2
-            if pair == 0:
-                tiles[name, h] = per_head.tile([P, PLANES, S, 2], BF16, name=name)
             bank = ps_words.tile([P, PLANES * PAIR], F32, name="word_bank")
-            transpose_words(nc, bank, rows, [2 * pair, 2 * pair + 1], ident_f32)
-            copy = nc.vector.tensor_copy if h == 0 and pair == 0 else nc.scalar.copy
-            copy(
-                out=tiles[name, h][:, :, pair * PAIR : (pair + 1) * PAIR, :]
-                .rearrange("p u r e -> p u (r e)")
-                .bitcast(F32),
-                in_=bank[:].rearrange("p (u r) -> p u r", u=PLANES),
-            )
+            copy = nc.vector.tensor_copy if h == 0 and quarter % 2 == 0 else nc.scalar.copy
+            if quarter < PLANES:
+                if quarter == 0:
+                    tiles["k_t", h] = per_head.tile([P, PLANES, S, 2], BF16, name="k_t")
+                words = k_rows[h][:].bitcast(F32)
+                for t in range(T):
+                    first_word = t * WORDS + quarter * P
+                    nc.tensor.transpose(
+                        bank[:, t * P : (t + 1) * P], words[:, first_word : first_word + P], ident_f32[:]
+                    )
+                copy(
+                    out=tiles["k_t", h][:, quarter, :, :]
+                    .rearrange("p j e -> p (j e)")
+                    .bitcast(F32)
+                    .rearrange("p (r t) -> p r t", t=T),
+                    in_=bank[:].rearrange("p (t r) -> p r t", t=T),
+                )
+            else:
+                pair = quarter - PLANES
+                if pair == 0:
+                    tiles["q_t", h] = per_head.tile([P, PLANES, S, 2], BF16, name="q_t")
+                transpose_words(nc, bank, q_rows[h], [2 * pair, 2 * pair + 1], ident_f32)
+                copy(
+                    out=tiles["q_t", h][:, :, pair * PAIR : (pair + 1) * PAIR, :]
+                    .rearrange("p u r e -> p u (r e)")
+                    .bitcast(F32),
+                    in_=bank[:].rearrange("p (u r) -> p u r", u=PLANES),
+                )
 
         def scores(n):
             if not 0 <= n < STEPS:
@@ -356,7 +359,10 @@ def tile_maskedmultiheadattention_pa_kernel(tc, q, k, value, mask, Wv, bv, out):
             h, t = divmod(n, T)
             o_sb = work.tile([P, V], F32, name="o_sb")
             nc.scalar.activation(
-                out=o_sb[:], in_=tiles["o_ps", n][:], func=ACT.Copy, scale=tiles["inv_sum", n][:]
+                out=o_sb[:].rearrange("p (r c) -> p r c", c=T),
+                in_=tiles["o_ps", n][:].rearrange("p (c r) -> p r c", c=T),
+                func=ACT.Copy,
+                scale=tiles["inv_sum", n][:],
             )
             nc.sync.dma_start(out=out_rows[:, t, h * V : (h + 1) * V], in_=o_sb[:])
 

@@ -27,18 +27,20 @@ PAIR = 2 * P
 SCALE = 1.0 / math.sqrt(D)
 STEPS = H * T
 
-QK = 4
-SCORES = 1
-WV_TRANSPOSE = 1
-WV_QUANTISE = 0
-PROJECT = -1
-BIAS = -2
-V_QUANTISE = -3
+QK = 5
+SCORES = 2
 EXP = -1
-E_TRANSPOSE = -2
-E_QUANTISE = -6
-EV = -7
-OUT = -7
+E_TRANSPOSE = -3
+E_QUANTISE = -4
+WV_TRANSPOSE = 0
+WV_QUANTISE = -2
+PROJECT = -2
+BIAS = -3
+V_QUANTISE = -5
+EV = -8
+OUT = -8
+
+WARM = 4
 
 FLOPS = 3 * H * 2 * S * D * V
 
@@ -76,6 +78,8 @@ def tile_maskedmultiheadattention_pa_kernel(tc, q, k, value, mask, Wv, bv, out):
         ps_et = ctx.enter_context(tc.psum_pool(name="ps_et", bufs=1))
         ps_mx = ctx.enter_context(tc.psum_pool(name="ps_mx", bufs=3))
 
+        ones = consts.tile([P, P], BF16)
+        nc.vector.memset(ones[:], 1.0)
         bias_row = consts.tile([P, H * V], BF16)
         nc.vector.memset(bias_row[:].bitcast(I32), 0)
 
@@ -95,9 +99,9 @@ def tile_maskedmultiheadattention_pa_kernel(tc, q, k, value, mask, Wv, bv, out):
             wv_rows.append(wv_sb)
         load_rows(k_rows[0], k[0], 0, T // 2)
         load_rows(k_rows[0], k[0], T // 2, T)
+        load_rows(q_rows[0], q[0], 0, 1)
         nc.sync.dma_start(out=bias_row[0:1, :], in_=bv.rearrange("h v -> (h v)").unsqueeze(0))
-        load_rows(q_rows[0], q[0], 0, T // 2)
-        load_rows(q_rows[0], q[0], T // 2, T)
+        load_rows(q_rows[0], q[0], 1, T)
         nc.sync.dma_start(out=mask_sb[:], in_=mask.rearrange("(p t) j -> p t j", t=T))
         nc.sync.dma_start(
             out=value_rows[:].rearrange("p (u x) -> p u x", u=PLANES),
@@ -112,8 +116,16 @@ def tile_maskedmultiheadattention_pa_kernel(tc, q, k, value, mask, Wv, bv, out):
 
         ident_f32 = consts.tile([P, P], F32)
         make_identity(nc, ident_f32[:])
-        ones = consts.tile([P, P], BF16)
-        nc.vector.memset(ones[:], 1.0)
+
+        warm_ps = ps_mx.tile([P, V], F32, name="mx_bank")
+        for i in range(WARM):
+            nc.tensor.matmul(
+                out=warm_ps[:],
+                lhsT=ones[:],
+                rhs=ones[:, 0:1].to_broadcast([P, V]),
+                start=True,
+                stop=True,
+            )
 
         table_warmer = consts.tile([P, 1], F32)
         nc.scalar.activation(out=table_warmer[:], in_=ones[:, 0:1], func=ACT.Exp)
@@ -123,7 +135,7 @@ def tile_maskedmultiheadattention_pa_kernel(tc, q, k, value, mask, Wv, bv, out):
         value_scales = consts.tile([P, S], U8, align_bytes=64)
 
         def transpose_value(pair):
-            bank = ps_words.tile([P, PLANES * PAIR], F32, name="word_bank")
+            bank = ps_mx.tile([P, PLANES * PAIR], F32, name="mx_bank")
             transpose_words(nc, bank, value_rows, [2 * pair, 2 * pair + 1], ident_f32)
             nc.scalar.copy(
                 out=as_words(value_grouped)[:, pair * PAIR : (pair + 1) * PAIR, :],
@@ -148,25 +160,26 @@ def tile_maskedmultiheadattention_pa_kernel(tc, q, k, value, mask, Wv, bv, out):
                     start=True,
                     stop=True,
                 )
-            nc.vector.tensor_copy(out=bias[:, 2 * pair * V : 2 * (pair + 1) * V], in_=bias_ps[:])
+            copy = nc.vector.tensor_copy if pair == 0 else nc.scalar.copy
+            copy(out=bias[:, 2 * pair * V : 2 * (pair + 1) * V], in_=bias_ps[:])
 
         tiles = {}
 
         def transpose_wv(m):
-            if not 0 <= m < STEPS:
+            if m % 2 or not 0 <= m < STEPS:
                 return
             h, c = divmod(m, T)
-            bank = ps_words.tile([P, PLANES * P], F32, name="word_bank")
-            transpose_words(nc, bank, wv_rows[h], [c], ident_f32)
-            grouped = work.tile([P, P * PACK], BF16, name="wv_grouped", align_bytes=64)
+            bank = ps_words.tile([P, PLANES * PAIR], F32, name="word_bank")
+            transpose_words(nc, bank, wv_rows[h], [c, c + 1], ident_f32)
+            grouped = work.tile([P, PAIR * PACK], BF16, name="wv_grouped", align_bytes=64)
             nc.scalar.copy(out=as_words(grouped), in_=planes_side_by_side(bank))
             tiles["wv_grouped", m] = grouped
 
         def quantise_wv(m):
-            if not 0 <= m < STEPS:
+            if m % 2 or not 0 <= m < STEPS:
                 return
-            codes = work.tile([P, P], U32, name="wv_codes", align_bytes=64)
-            scales = work.tile([P, P], U8, name="wv_scales", align_bytes=64)
+            codes = work.tile([P, PAIR], U32, name="wv_codes", align_bytes=64)
+            scales = work.tile([P, PAIR], U8, name="wv_scales", align_bytes=64)
             nc.vector.quantize_mx(
                 out=codes[:].bitcast(FP8X4), scales=scales[:], in_=tiles["wv_grouped", m][:]
             )
@@ -177,14 +190,16 @@ def tile_maskedmultiheadattention_pa_kernel(tc, q, k, value, mask, Wv, bv, out):
             if not 0 <= m < STEPS:
                 return
             v_ps = ps_mx.tile([P, T, P], F32, name="mx_bank")
+            pair = m - m % 2
+            cols = slice(m % 2 * P, (m % 2 + 1) * P)
             for t in range(T):
                 keys = slice(t * P, (t + 1) * P)
                 nc.tensor.matmul_mx(
                     out=v_ps[:, t, :],
                     lhsT=value_codes[:, keys].bitcast(FP8X4),
                     lhsT_scale=value_scales[:, keys],
-                    rhs=tiles["wv_codes", m][:].bitcast(FP8X4),
-                    rhs_scale=tiles["wv_scales", m][:],
+                    rhs=tiles["wv_codes", pair][:, cols].bitcast(FP8X4),
+                    rhs_scale=tiles["wv_scales", pair][:, cols],
                     start=True,
                     stop=True,
                 )
@@ -209,49 +224,55 @@ def tile_maskedmultiheadattention_pa_kernel(tc, q, k, value, mask, Wv, bv, out):
             )
 
         def quantise_v(m):
-            if not 0 <= m < STEPS:
+            if m % 2 or not 0 <= m < STEPS:
                 return
             h, c = divmod(m, T)
-            cols = slice(c * P, (c + 1) * P)
+            cols = slice(c * P, c * P + PAIR)
             nc.vector.quantize_mx(
                 out=tiles["v_codes", h][:, cols].bitcast(FP8X4),
                 scales=tiles["v_scales", h][:, cols],
                 in_=tiles["v_grouped", h][:, cols, :].rearrange("p c t -> p (c t)"),
             )
 
+        def transpose_k(h, u, copy):
+            if u == 0:
+                tiles["k_t", h] = per_head.tile([P, PLANES, S, 2], BF16, name="k_t")
+            bank = ps_words.tile([P, T * P], F32, name="word_bank")
+            words = k_rows[h][:].bitcast(F32)
+            for t in range(T):
+                first_word = t * WORDS + u * P
+                nc.tensor.transpose(
+                    bank[:, t * P : (t + 1) * P], words[:, first_word : first_word + P], ident_f32[:]
+                )
+            copy(
+                out=tiles["k_t", h][:, u, :, :]
+                .rearrange("p j e -> p (j e)")
+                .bitcast(F32)
+                .rearrange("p (r t) -> p r t", t=T),
+                in_=bank[:].rearrange("p (t r) -> p r t", t=T),
+            )
+
+        def transpose_q(h, first, last, bank, copy):
+            if first == 0:
+                tiles["q_t", h] = per_head.tile([P, PLANES, S, 2], BF16, name="q_t")
+            transpose_words(nc, bank, q_rows[h], list(range(first, last)), ident_f32)
+            copy(
+                out=tiles["q_t", h][:, :, first * P : last * P, :]
+                .rearrange("p u r e -> p u (r e)")
+                .bitcast(F32),
+                in_=bank[:].rearrange("p (u r) -> p u r", u=PLANES),
+            )
+
         def transpose_qk(m):
-            if not 0 <= m < STEPS:
+            if not T <= m < STEPS:
                 return
             h, quarter = divmod(m, T)
-            bank = ps_words.tile([P, PLANES * PAIR], F32, name="word_bank")
-            copy = nc.vector.tensor_copy if h == 0 and quarter % 2 == 0 else nc.scalar.copy
             if quarter < PLANES:
-                if quarter == 0:
-                    tiles["k_t", h] = per_head.tile([P, PLANES, S, 2], BF16, name="k_t")
-                words = k_rows[h][:].bitcast(F32)
-                for t in range(T):
-                    first_word = t * WORDS + quarter * P
-                    nc.tensor.transpose(
-                        bank[:, t * P : (t + 1) * P], words[:, first_word : first_word + P], ident_f32[:]
-                    )
-                copy(
-                    out=tiles["k_t", h][:, quarter, :, :]
-                    .rearrange("p j e -> p (j e)")
-                    .bitcast(F32)
-                    .rearrange("p (r t) -> p r t", t=T),
-                    in_=bank[:].rearrange("p (t r) -> p r t", t=T),
-                )
+                transpose_k(h, quarter, nc.scalar.copy)
             else:
-                pair = quarter - PLANES
-                if pair == 0:
-                    tiles["q_t", h] = per_head.tile([P, PLANES, S, 2], BF16, name="q_t")
-                transpose_words(nc, bank, q_rows[h], [2 * pair, 2 * pair + 1], ident_f32)
-                copy(
-                    out=tiles["q_t", h][:, :, pair * PAIR : (pair + 1) * PAIR, :]
-                    .rearrange("p u r e -> p u (r e)")
-                    .bitcast(F32),
-                    in_=bank[:].rearrange("p (u r) -> p u r", u=PLANES),
-                )
+                first = 2 * (quarter - PLANES)
+                bank = ps_words.tile([P, PLANES * PAIR], F32, name="word_bank")
+                transpose_q(h, first, first + 2, bank, nc.scalar.copy)
 
         def scores(n):
             if not 0 <= n < STEPS:
@@ -296,39 +317,45 @@ def tile_maskedmultiheadattention_pa_kernel(tc, q, k, value, mask, Wv, bv, out):
             if not 0 <= n < STEPS:
                 return
             e_sb = work.tile([P, S], BF16, name="e_sb")
-            row_sum = work.tile([P, 1], F32, name="row_sum")
+            h, t = divmod(n, T)
+            if t == 0:
+                tiles["row_sum", h] = work.tile([P, T], F32, name="row_sum")
             nc.scalar.activation(
                 out=e_sb[:],
                 in_=tiles["masked", n][:],
                 func=ACT.Exp,
                 bias=tiles["neg_max", n][:],
                 scale=1.0,
-                accum_out=row_sum[:],
+                accum_out=tiles["row_sum", h][:, t : t + 1],
             )
             tiles["e_sb", n] = e_sb
-            tiles["row_sum", n] = row_sum
 
         def reciprocal(n):
-            if not 0 <= n < STEPS:
+            if n % T or not 0 <= n < STEPS:
                 return
-            inv_sum = work.tile([P, 1], F32, name="inv_sum")
-            nc.vector.reciprocal(out=inv_sum[:], in_=tiles["row_sum", n][:])
-            tiles["inv_sum", n] = inv_sum
+            h = n // T
+            inv_sum = work.tile([P, T], F32, name="inv_sum")
+            nc.vector.reciprocal(out=inv_sum[:], in_=tiles["row_sum", h][:])
+            tiles["inv_sum", h] = inv_sum
 
         def transpose_e(n):
-            if not 0 <= n < STEPS:
+            if n % 2 or not 0 <= n < STEPS:
                 return
-            et_ps = ps_et.tile([P, PLANES * P], F32, name="et_ps")
-            transpose_words(nc, et_ps, tiles["e_sb", n], [0], ident_f32)
-            e_grouped = work.tile([P, P * PACK], BF16, name="e_grouped", align_bytes=64)
-            nc.scalar.copy(out=as_words(e_grouped), in_=planes_side_by_side(et_ps))
+            et_ps = ps_et.tile([P, 2, PLANES * P], F32, name="et_ps")
+            for i in range(2):
+                transpose_words(nc, et_ps[:, i, :], tiles["e_sb", n + i], [0], ident_f32)
+            e_grouped = work.tile([P, PAIR * PACK], BF16, name="e_grouped", align_bytes=64)
+            nc.scalar.copy(
+                out=e_grouped[:].bitcast(F32).rearrange("p (i r u) -> p i r u", i=2, u=PLANES),
+                in_=et_ps[:].rearrange("p i (u r) -> p i r u", u=PLANES),
+            )
             tiles["e_grouped", n] = e_grouped
 
         def quantise_e(n):
-            if not 0 <= n < STEPS:
+            if n % 2 or not 0 <= n < STEPS:
                 return
-            codes = work.tile([P, P], U32, name="e_codes", align_bytes=64)
-            scales = work.tile([P, P], U8, name="e_scales", align_bytes=64)
+            codes = work.tile([P, PAIR], U32, name="e_codes", align_bytes=64)
+            scales = work.tile([P, PAIR], U8, name="e_scales", align_bytes=64)
             nc.vector.quantize_mx(
                 out=codes[:].bitcast(FP8X4),
                 scales=scales[:],
@@ -341,11 +368,12 @@ def tile_maskedmultiheadattention_pa_kernel(tc, q, k, value, mask, Wv, bv, out):
             if not 0 <= n < STEPS:
                 return
             h = n // T
+            rows = slice(n % 2 * P, (n % 2 + 1) * P)
             o_ps = ps_mx.tile([P, V], F32, name="mx_bank")
             nc.tensor.matmul_mx(
                 out=o_ps[:],
-                lhsT=tiles["e_codes", n][:].bitcast(FP8X4),
-                lhsT_scale=tiles["e_scales", n][:],
+                lhsT=tiles["e_codes", n - n % 2][:, rows].bitcast(FP8X4),
+                lhsT_scale=tiles["e_scales", n - n % 2][:, rows],
                 rhs=tiles["v_codes", h][:].bitcast(FP8X4),
                 rhs_scale=tiles["v_scales", h][:],
                 start=True,
@@ -358,37 +386,60 @@ def tile_maskedmultiheadattention_pa_kernel(tc, q, k, value, mask, Wv, bv, out):
                 return
             h, t = divmod(n, T)
             o_sb = work.tile([P, V], F32, name="o_sb")
-            nc.scalar.activation(
-                out=o_sb[:].rearrange("p (r c) -> p r c", c=T),
-                in_=tiles["o_ps", n][:].rearrange("p (c r) -> p r c", c=T),
-                func=ACT.Copy,
-                scale=tiles["inv_sum", n][:],
-            )
+            if h == H - 1 and t % 2 == 1:
+                nc.vector.tensor_scalar(
+                    out=o_sb[:].rearrange("p (r c) -> p r c", c=T),
+                    in0=tiles["o_ps", n][:].rearrange("p (c r) -> p r c", c=T),
+                    scalar1=tiles["inv_sum", h][:, t : t + 1],
+                    scalar2=None,
+                    op0=ALU.mult,
+                )
+            else:
+                nc.scalar.activation(
+                    out=o_sb[:].rearrange("p (r c) -> p r c", c=T),
+                    in_=tiles["o_ps", n][:].rearrange("p (c r) -> p r c", c=T),
+                    func=ACT.Copy,
+                    scale=tiles["inv_sum", h][:, t : t + 1],
+                )
             nc.sync.dma_start(out=out_rows[:, t, h * V : (h + 1) * V], in_=o_sb[:])
 
-        for step in range(-QK, STEPS - OUT):
-            exponential(step + EXP)
-            if step == -1:
-                spread_bias(1)
-            quantise_e(step + E_QUANTISE)
-            quantise_v(step + V_QUANTISE)
+        transpose_k(0, 0, nc.vector.tensor_copy)
+        transpose_k(0, 1, nc.scalar.copy)
+        bank = ps_mx.tile([P, PLANES * P], F32, name="mx_bank")
+        transpose_q(0, 0, 1, bank, nc.vector.tensor_copy)
+        spread_bias(0)
+        bank = ps_mx.tile([P, PLANES * P], F32, name="mx_bank")
+        transpose_q(0, 1, 2, bank, nc.scalar.copy)
+        scores(0)
+        bank = ps_words.tile([P, PLANES * PAIR], F32, name="word_bank")
+        transpose_q(0, 2, T, bank, nc.scalar.copy)
+        scores(1)
+        transpose_value(0)
+        transpose_value(1)
+
+        for step in range(STEPS - OUT):
             apply_mask(step)
-            if step == -1:
-                transpose_value(0)
-            multiply_e_v(step + EV)
-            if step == 0:
-                quantise_value()
-            if step == -3:
-                spread_bias(0)
-            divide_and_store(step + OUT)
-            if step == -1:
-                transpose_value(1)
-            scores(step + SCORES)
-            add_bias(step + BIAS)
-            transpose_qk(step + QK)
-            reciprocal(step + E_QUANTISE)
-            transpose_wv(step + WV_TRANSPOSE)
             transpose_e(step + E_TRANSPOSE)
-            project_v(step + PROJECT)
-            row_max(step)
+            transpose_wv(step + WV_TRANSPOSE)
+            if step == 1:
+                transpose_qk(step + QK - 2)
+                transpose_qk(step + QK - 1)
+            if step >= 1:
+                transpose_qk(step + QK)
             quantise_wv(step + WV_QUANTISE)
+            add_bias(step + BIAS)
+            quantise_v(step + V_QUANTISE)
+            row_max(step)
+            exponential(step + EXP)
+            quantise_e(step + E_QUANTISE)
+            reciprocal(step + E_QUANTISE - 1)
+            multiply_e_v(step + EV)
+            if (step + PROJECT) % 2 == 0:
+                project_v(step + PROJECT)
+                project_v(step + PROJECT + 1)
+            divide_and_store(step + OUT)
+            if step == 1:
+                quantise_value()
+            if step == T:
+                spread_bias(1)
+            scores(step + SCORES)

@@ -31,14 +31,14 @@ QK = 5
 SCORES = 2
 EXP = -1
 E_TRANSPOSE = -3
-E_QUANTISE = -4
+E_QUANTISE = -5
 WV_TRANSPOSE = 0
-WV_QUANTISE = -2
+WV_QUANTISE = -1
 PROJECT = -2
 BIAS = -3
-V_QUANTISE = -5
-EV = -8
-OUT = -8
+V_QUANTISE = -4
+EV = -7
+OUT = -7
 
 WARM = 4
 
@@ -386,21 +386,12 @@ def tile_maskedmultiheadattention_pa_kernel(tc, q, k, value, mask, Wv, bv, out):
                 return
             h, t = divmod(n, T)
             o_sb = work.tile([P, V], F32, name="o_sb")
-            if h == H - 1 and t % 2 == 1:
-                nc.vector.tensor_scalar(
-                    out=o_sb[:].rearrange("p (r c) -> p r c", c=T),
-                    in0=tiles["o_ps", n][:].rearrange("p (c r) -> p r c", c=T),
-                    scalar1=tiles["inv_sum", h][:, t : t + 1],
-                    scalar2=None,
-                    op0=ALU.mult,
-                )
-            else:
-                nc.scalar.activation(
-                    out=o_sb[:].rearrange("p (r c) -> p r c", c=T),
-                    in_=tiles["o_ps", n][:].rearrange("p (c r) -> p r c", c=T),
-                    func=ACT.Copy,
-                    scale=tiles["inv_sum", h][:, t : t + 1],
-                )
+            nc.scalar.activation(
+                out=o_sb[:].rearrange("p (r c) -> p r c", c=T),
+                in_=tiles["o_ps", n][:].rearrange("p (c r) -> p r c", c=T),
+                func=ACT.Copy,
+                scale=tiles["inv_sum", h][:, t : t + 1],
+            )
             nc.sync.dma_start(out=out_rows[:, t, h * V : (h + 1) * V], in_=o_sb[:])
 
         transpose_k(0, 0, nc.vector.tensor_copy)
@@ -410,36 +401,34 @@ def tile_maskedmultiheadattention_pa_kernel(tc, q, k, value, mask, Wv, bv, out):
         spread_bias(0)
         bank = ps_mx.tile([P, PLANES * P], F32, name="mx_bank")
         transpose_q(0, 1, 2, bank, nc.scalar.copy)
-        scores(0)
         bank = ps_words.tile([P, PLANES * PAIR], F32, name="word_bank")
         transpose_q(0, 2, T, bank, nc.scalar.copy)
+        scores(0)
         scores(1)
         transpose_value(0)
         transpose_value(1)
 
         for step in range(STEPS - OUT):
+            exponential(step + EXP)
             apply_mask(step)
-            transpose_e(step + E_TRANSPOSE)
             transpose_wv(step + WV_TRANSPOSE)
             if step == 1:
                 transpose_qk(step + QK - 2)
                 transpose_qk(step + QK - 1)
             if step >= 1:
                 transpose_qk(step + QK)
-            quantise_wv(step + WV_QUANTISE)
+            project_v(step + PROJECT)
+            transpose_e(step + E_TRANSPOSE)
             add_bias(step + BIAS)
-            quantise_v(step + V_QUANTISE)
-            row_max(step)
-            exponential(step + EXP)
             quantise_e(step + E_QUANTISE)
-            reciprocal(step + E_QUANTISE - 1)
             multiply_e_v(step + EV)
-            if (step + PROJECT) % 2 == 0:
-                project_v(step + PROJECT)
-                project_v(step + PROJECT + 1)
+            reciprocal(step + OUT)
             divide_and_store(step + OUT)
-            if step == 1:
-                quantise_value()
-            if step == T:
+            row_max(step)
+            if step == 5:
                 spread_bias(1)
             scores(step + SCORES)
+            quantise_v(step + V_QUANTISE)
+            if step == 1:
+                quantise_value()
+            quantise_wv(step + WV_QUANTISE)

@@ -27,11 +27,11 @@ PAIR = 2 * P
 SCALE = 1.0 / math.sqrt(D)
 STEPS = H * T
 
-QK = 5
+QK = 4
 SCORES = 2
 EXP = -1
 E_TRANSPOSE = -3
-E_QUANTISE = -5
+E_QUANTISE = -6
 WV_TRANSPOSE = 0
 WV_QUANTISE = -1
 PROJECT = -2
@@ -411,12 +411,11 @@ def tile_maskedmultiheadattention_pa_kernel(tc, q, k, value, mask, Wv, bv, out):
         for step in range(STEPS - OUT):
             exponential(step + EXP)
             apply_mask(step)
-            transpose_wv(step + WV_TRANSPOSE)
             if step == 1:
-                transpose_qk(step + QK - 2)
-                transpose_qk(step + QK - 1)
+                transpose_qk(T)
             if step >= 1:
                 transpose_qk(step + QK)
+            transpose_wv(step + WV_TRANSPOSE)
             project_v(step + PROJECT)
             transpose_e(step + E_TRANSPOSE)
             add_bias(step + BIAS)
@@ -425,7 +424,7 @@ def tile_maskedmultiheadattention_pa_kernel(tc, q, k, value, mask, Wv, bv, out):
             reciprocal(step + OUT)
             divide_and_store(step + OUT)
             row_max(step)
-            if step == 5:
+            if step == 6:
                 spread_bias(1)
             scores(step + SCORES)
             quantise_v(step + V_QUANTISE)

@@ -409,12 +409,12 @@ def tile_maskedmultiheadattention_pa_kernel(tc, q, k, value, mask, Wv, bv, out):
         transpose_value(1)
 
         for step in range(STEPS - OUT):
-            exponential(step + EXP)
             apply_mask(step)
             if step == 1:
                 transpose_qk(T)
             if step >= 1:
                 transpose_qk(step + QK)
+            exponential(step + EXP)
             transpose_wv(step + WV_TRANSPOSE)
             project_v(step + PROJECT)
             transpose_e(step + E_TRANSPOSE)

@@ -97,17 +97,29 @@ def tile_maskedmultiheadattention_pa_kernel(tc, q, k, value, mask, Wv, bv, out):
             q_rows.append(q_sb)
             wv_sb = per_head.tile([P, T * D], BF16)
             wv_rows.append(wv_sb)
-        load_rows(k_rows[0], k[0], 0, T // 2)
-        load_rows(k_rows[0], k[0], T // 2, T)
+        def load_k_tile(t):
+            nc.sync.dma_start(out=k_rows[0][:, t * D : (t + 1) * D], in_=k[0, t * P : (t + 1) * P, :])
+
+        def load_mask(first, last):
+            nc.sync.dma_start(
+                out=mask_sb[:, first:last, :],
+                in_=mask.rearrange("(p t) j -> p t j", t=T)[:, first:last, :],
+            )
+
         load_rows(q_rows[0], q[0], 0, 1)
+        load_k_tile(0)
+        load_k_tile(1)
+        load_k_tile(2)
+        load_k_tile(3)
         nc.sync.dma_start(out=bias_row[0:1, :], in_=bv.rearrange("h v -> (h v)").unsqueeze(0))
+        load_mask(0, 1)
         load_rows(q_rows[0], q[0], 1, T)
-        nc.sync.dma_start(out=mask_sb[:], in_=mask.rearrange("(p t) j -> p t j", t=T))
         nc.sync.dma_start(
             out=value_rows[:].rearrange("p (u x) -> p u x", u=PLANES),
             in_=value.rearrange("(u p e) d -> p u (e d)", u=PLANES, e=2),
         )
         load_rows(wv_rows[0], Wv[0])
+        load_mask(1, T)
         for h in range(1, H):
             load_rows(k_rows[h], k[h])
             load_rows(q_rows[h], q[h])
@@ -252,12 +264,12 @@ def tile_maskedmultiheadattention_pa_kernel(tc, q, k, value, mask, Wv, bv, out):
                 in_=bank[:].rearrange("p (t r) -> p r t", t=T),
             )
 
-        def transpose_q(h, first, last, bank, copy):
+        def transpose_rows(name, rows, h, first, last, bank, copy):
             if first == 0:
-                tiles["q_t", h] = per_head.tile([P, PLANES, S, 2], BF16, name="q_t")
-            transpose_words(nc, bank, q_rows[h], list(range(first, last)), ident_f32)
+                tiles[name, h] = per_head.tile([P, PLANES, S, 2], BF16, name=name)
+            transpose_words(nc, bank, rows[h], list(range(first, last)), ident_f32)
             copy(
-                out=tiles["q_t", h][:, :, first * P : last * P, :]
+                out=tiles[name, h][:, :, first * P : last * P, :]
                 .rearrange("p u r e -> p u (r e)")
                 .bitcast(F32),
                 in_=bank[:].rearrange("p (u r) -> p u r", u=PLANES),
@@ -272,23 +284,28 @@ def tile_maskedmultiheadattention_pa_kernel(tc, q, k, value, mask, Wv, bv, out):
             else:
                 first = 2 * (quarter - PLANES)
                 bank = ps_words.tile([P, PLANES * PAIR], F32, name="word_bank")
-                transpose_q(h, first, first + 2, bank, nc.scalar.copy)
+                transpose_rows("q_t", q_rows, h, first, first + 2, bank, nc.scalar.copy)
 
-        def scores(n):
+        def scores(n, parts=1):
             if not 0 <= n < STEPS:
                 return
+            for part in range(parts):
+                scores_part(n, part, parts)
+
+        def scores_part(n, part, parts):
             h, t = divmod(n, T)
-            s_ps = ps_scores.tile([P, S], F32, name="s_ps")
+            if part == 0:
+                tiles["s_ps", n] = ps_scores.tile([P, S], F32, name="s_ps")
+            keys = slice(part * S // parts, (part + 1) * S // parts)
             for u in range(PLANES):
                 for e in range(2):
                     nc.tensor.matmul(
-                        out=s_ps[:],
+                        out=tiles["s_ps", n][:, keys],
                         lhsT=tiles["q_t", h][:, u, t * P : (t + 1) * P, e],
-                        rhs=tiles["k_t", h][:, u, :, e],
+                        rhs=tiles["k_t", h][:, u, keys, e],
                         start=(u == 0 and e == 0),
                         stop=(u == PLANES - 1 and e == 1),
                     )
-            tiles["s_ps", n] = s_ps
 
         def apply_mask(n):
             if not 0 <= n < STEPS:
@@ -394,19 +411,28 @@ def tile_maskedmultiheadattention_pa_kernel(tc, q, k, value, mask, Wv, bv, out):
             )
             nc.sync.dma_start(out=out_rows[:, t, h * V : (h + 1) * V], in_=o_sb[:])
 
-        transpose_k(0, 0, nc.vector.tensor_copy)
-        transpose_k(0, 1, nc.scalar.copy)
         bank = ps_mx.tile([P, PLANES * P], F32, name="mx_bank")
-        transpose_q(0, 0, 1, bank, nc.vector.tensor_copy)
+        transpose_rows("q_t", q_rows, 0, 0, 1, bank, nc.vector.tensor_copy)
+        bank = ps_mx.tile([P, PLANES * P], F32, name="mx_bank")
+        transpose_rows("k_t", k_rows, 0, 0, 1, bank, nc.scalar.copy)
+        bank = ps_words.tile([P, PLANES * P], F32, name="word_bank")
+        transpose_rows("k_t", k_rows, 0, 1, 2, bank, nc.vector.tensor_copy)
+        bank = ps_words.tile([P, PLANES * P], F32, name="word_bank")
+        transpose_rows("k_t", k_rows, 0, 2, 3, bank, nc.vector.tensor_copy)
         spread_bias(0)
+        scores_part(0, 0, T)
         bank = ps_mx.tile([P, PLANES * P], F32, name="mx_bank")
-        transpose_q(0, 1, 2, bank, nc.scalar.copy)
+        transpose_rows("k_t", k_rows, 0, 3, 4, bank, nc.vector.tensor_copy)
+        scores_part(0, 1, T)
         bank = ps_words.tile([P, PLANES * PAIR], F32, name="word_bank")
-        transpose_q(0, 2, T, bank, nc.scalar.copy)
-        scores(0)
-        scores(1)
-        transpose_value(0)
+        transpose_rows("q_t", q_rows, 0, 2, 4, bank, nc.vector.tensor_copy)
+        bank = ps_words.tile([P, PLANES * P], F32, name="word_bank")
+        transpose_rows("q_t", q_rows, 0, 1, 2, bank, nc.scalar.copy)
+        scores_part(0, 2, T)
+        scores_part(0, 3, T)
         transpose_value(1)
+        transpose_value(0)
+        scores(1)
 
         for step in range(STEPS - OUT):
             apply_mask(step)

import math
from contextlib import ExitStack

import concourse.mybir as mybir
from concourse.masks import make_identity

BF16 = mybir.dt.bfloat16
F32 = mybir.dt.float32
I32 = mybir.dt.int32
U32 = mybir.dt.uint32
U8 = mybir.dt.uint8
FP8X4 = mybir.dt.float8_e4m3fn_x4
ALU = mybir.AluOpType
ACT = mybir.ActivationFunctionType
AXIS = mybir.AxisListType

P = 128
H = 4
S = 512
D = 512
V = 512
T = S // P
PACK = 4
WORDS = D // 2
PLANES = WORDS // P
PAIR = 2 * P
SCALE = 1.0 / math.sqrt(D)
STEPS = H * T

QK = 4
SCORES = 2
EXP = -1
E_TRANSPOSE = -3
E_QUANTISE = -6
WV_TRANSPOSE = 0
WV_QUANTISE = -1
PROJECT = -2
BIAS = -3
V_QUANTISE = -4
EV = -7
OUT = -7

WARM = 4

FLOPS = 3 * H * 2 * S * D * V


def transpose_words(nc, bank, rows, row_tiles, ident_f32):
    words = rows[:].bitcast(F32)
    n = len(row_tiles)
    for u in range(PLANES):
        for i in range(n):
            first_word = row_tiles[i] * WORDS + u * P
            nc.tensor.transpose(
                bank[:, (u * n + i) * P : (u * n + i + 1) * P],
                words[:, first_word : first_word + P],
                ident_f32[:],
            )


def planes_side_by_side(bank):
    return bank[:].rearrange("p (u r) -> p r u", u=PLANES)


def as_words(grouped):
    return grouped[:].bitcast(F32).rearrange("p (r u) -> p r u", u=PLANES)


def tile_maskedmultiheadattention_pa_kernel(tc, q, k, value, mask, Wv, bv, out):
    nc = tc.nc
    with ExitStack() as ctx:
        ctx.enter_context(tc.manual_schedule())
        consts = ctx.enter_context(tc.tile_pool(name="consts", bufs=1))
        per_head = ctx.enter_context(tc.tile_pool(name="per_head", bufs=H))
        work = ctx.enter_context(tc.tile_pool(name="work", bufs=8))
        ps_words = ctx.enter_context(tc.psum_pool(name="ps_words", bufs=2))
        ps_scores = ctx.enter_context(tc.psum_pool(name="ps_scores", bufs=2))
        ps_et = ctx.enter_context(tc.psum_pool(name="ps_et", bufs=1))
        ps_mx = ctx.enter_context(tc.psum_pool(name="ps_mx", bufs=3))

        ones = consts.tile([P, P], BF16)
        nc.vector.memset(ones[:], 1.0)
        bias_row = consts.tile([P, H * V], BF16)
        nc.vector.memset(bias_row[:].bitcast(I32), 0)

        def load_rows(rows_sb, rows, first=0, last=T):
            cols = slice(first * D, last * D)
            nc.sync.dma_start(out=rows_sb[:, cols], in_=rows.rearrange("(p t) d -> p (t d)", t=T)[:, cols])

        value_rows = consts.tile([P, T * D], BF16)
        mask_sb = consts.tile([P, T, S], BF16)
        k_rows, q_rows, wv_rows = [], [], []
        for h in range(H):
            k_sb = per_head.tile([P, T * D], BF16)
            k_rows.append(k_sb)
            q_sb = per_head.tile([P, T * D], BF16)
            q_rows.append(q_sb)
            wv_sb = per_head.tile([P, T * D], BF16)
            wv_rows.append(wv_sb)
        def load_k_tile(t):
            nc.sync.dma_start(out=k_rows[0][:, t * D : (t + 1) * D], in_=k[0, t * P : (t + 1) * P, :])

        def load_mask(first, last):
            nc.sync.dma_start(
                out=mask_sb[:, first:last, :],
                in_=mask.rearrange("(p t) j -> p t j", t=T)[:, first:last, :],
            )

        load_rows(q_rows[0], q[0], 0, 1)
        load_k_tile(0)
        load_k_tile(1)
        load_k_tile(2)
        load_k_tile(3)
        nc.sync.dma_start(out=bias_row[0:1, :], in_=bv.rearrange("h v -> (h v)").unsqueeze(0))
        load_mask(0, 1)
        load_rows(q_rows[0], q[0], 1, T)
        nc.sync.dma_start(
            out=value_rows[:].rearrange("p (u x) -> p u x", u=PLANES),
            in_=value.rearrange("(u p e) d -> p u (e d)", u=PLANES, e=2),
        )
        load_rows(wv_rows[0], Wv[0])
        load_mask(1, T)
        for h in range(1, H):
            load_rows(k_rows[h], k[h])
            load_rows(q_rows[h], q[h])
            load_rows(wv_rows[h], Wv[h])
        out_rows = out.rearrange("(p t) c -> p t c", t=T)

        ident_f32 = consts.tile([P, P], F32)
        make_identity(nc, ident_f32[:])

        warm_ps = ps_mx.tile([P, V], F32, name="mx_bank")
        for i in range(WARM):
            nc.tensor.matmul(
                out=warm_ps[:],
                lhsT=ones[:],
                rhs=ones[:, 0:1].to_broadcast([P, V]),
                start=True,
                stop=True,
            )

        table_warmer = consts.tile([P, 1], F32)
        nc.scalar.activation(out=table_warmer[:], in_=ones[:, 0:1], func=ACT.Exp)

        value_grouped = consts.tile([P, S * PACK], BF16, align_bytes=64)
        value_codes = consts.tile([P, S], U32, align_bytes=64)
        value_scales = consts.tile([P, S], U8, align_bytes=64)

        def transpose_value(pair):
            bank = ps_mx.tile([P, PLANES * PAIR], F32, name="mx_bank")
            transpose_words(nc, bank, value_rows, [2 * pair, 2 * pair + 1], ident_f32)
            nc.scalar.copy(
                out=as_words(value_grouped)[:, pair * PAIR : (pair + 1) * PAIR, :],
                in_=planes_side_by_side(bank),
            )

        def quantise_value():
            nc.vector.quantize_mx(
                out=value_codes[:].bitcast(FP8X4), scales=value_scales[:], in_=value_grouped[:]
            )

        bias = consts.tile([P, H * V], BF16)

        def spread_bias(pair):
            bias_ps = ps_mx.tile([P, 2 * V], BF16, name="mx_bank")
            for i in range(2):
                h = 2 * pair + i
                nc.tensor.matmul(
                    out=bias_ps[:, i * V : (i + 1) * V],
                    lhsT=ones[:],
                    rhs=bias_row[:, h * V : (h + 1) * V],
                    start=True,
                    stop=True,
                )
            copy = nc.vector.tensor_copy if pair == 0 else nc.scalar.copy
            copy(out=bias[:, 2 * pair * V : 2 * (pair + 1) * V], in_=bias_ps[:])

        tiles = {}

        def transpose_wv(m):
            if m % 2 or not 0 <= m < STEPS:
                return
            h, c = divmod(m, T)
            bank = ps_words.tile([P, PLANES * PAIR], F32, name="word_bank")
            transpose_words(nc, bank, wv_rows[h], [c, c + 1], ident_f32)
            grouped = work.tile([P, PAIR * PACK], BF16, name="wv_grouped", align_bytes=64)
            nc.scalar.copy(out=as_words(grouped), in_=planes_side_by_side(bank))
            tiles["wv_grouped", m] = grouped

        def quantise_wv(m):
            if m % 2 or not 0 <= m < STEPS:
                return
            codes = work.tile([P, PAIR], U32, name="wv_codes", align_bytes=64)
            scales = work.tile([P, PAIR], U8, name="wv_scales", align_bytes=64)
            nc.vector.quantize_mx(
                out=codes[:].bitcast(FP8X4), scales=scales[:], in_=tiles["wv_grouped", m][:]
            )
            tiles["wv_codes", m] = codes
            tiles["wv_scales", m] = scales

        def project_v(m):
            if not 0 <= m < STEPS:
                return
            v_ps = ps_mx.tile([P, T, P], F32, name="mx_bank")
            pair = m - m % 2
            cols = slice(m % 2 * P, (m % 2 + 1) * P)
            for t in range(T):
                keys = slice(t * P, (t + 1) * P)
                nc.tensor.matmul_mx(
                    out=v_ps[:, t, :],
                    lhsT=value_codes[:, keys].bitcast(FP8X4),
                    lhsT_scale=value_scales[:, keys],
                    rhs=tiles["wv_codes", pair][:, cols].bitcast(FP8X4),
                    rhs_scale=tiles["wv_scales", pair][:, cols],
                    start=True,
                    stop=True,
                )
            tiles["v_ps", m] = v_ps

        def add_bias(m):
            if not 0 <= m < STEPS:
                return
            h, c = divmod(m, T)
            if c == 0:
                tiles["v_grouped", h] = per_head.tile([P, V, PACK], BF16, name="v_grouped", align_bytes=64)
                tiles["v_codes", h] = per_head.tile([P, V], U32, name="v_codes", align_bytes=64)
                tiles["v_scales", h] = per_head.tile([P, V], U8, name="v_scales", align_bytes=64)
            nc.vector.tensor_tensor(
                out=tiles["v_grouped", h][:, c * P : (c + 1) * P, :],
                in0=tiles["v_ps", m][:].rearrange("p t c -> p c t"),
                in1=bias[:, h * V : (h + 1) * V]
                .rearrange("p (r c) -> p r c", c=T)[:, :, c]
                .unsqueeze(2)
                .to_broadcast([P, P, T]),
                op=ALU.add,
            )

        def quantise_v(m):
            if m % 2 or not 0 <= m < STEPS:
                return
            h, c = divmod(m, T)
            cols = slice(c * P, c * P + PAIR)
            nc.vector.quantize_mx(
                out=tiles["v_codes", h][:, cols].bitcast(FP8X4),
                scales=tiles["v_scales", h][:, cols],
                in_=tiles["v_grouped", h][:, cols, :].rearrange("p c t -> p (c t)"),
            )

        def transpose_k(h, u, copy):
            if u == 0:
                tiles["k_t", h] = per_head.tile([P, PLANES, S, 2], BF16, name="k_t")
            bank = ps_words.tile([P, T * P], F32, name="word_bank")
            words = k_rows[h][:].bitcast(F32)
            for t in range(T):
                first_word = t * WORDS + u * P
                nc.tensor.transpose(
                    bank[:, t * P : (t + 1) * P], words[:, first_word : first_word + P], ident_f32[:]
                )
            copy(
                out=tiles["k_t", h][:, u, :, :]
                .rearrange("p j e -> p (j e)")
                .bitcast(F32)
                .rearrange("p (r t) -> p r t", t=T),
                in_=bank[:].rearrange("p (t r) -> p r t", t=T),
            )

        def transpose_rows(name, rows, h, first, last, bank, copy):
            if first == 0:
                tiles[name, h] = per_head.tile([P, PLANES, S, 2], BF16, name=name)
            transpose_words(nc, bank, rows[h], list(range(first, last)), ident_f32)
            copy(
                out=tiles[name, h][:, :, first * P : last * P, :]
                .rearrange("p u r e -> p u (r e)")
                .bitcast(F32),
                in_=bank[:].rearrange("p (u r) -> p u r", u=PLANES),
            )

        def transpose_qk(m):
            if not T <= m < STEPS:
                return
            h, quarter = divmod(m, T)
            if quarter < PLANES:
                transpose_k(h, quarter, nc.scalar.copy)
            else:
                first = 2 * (quarter - PLANES)
                bank = ps_words.tile([P, PLANES * PAIR], F32, name="word_bank")
                transpose_rows("q_t", q_rows, h, first, first + 2, bank, nc.scalar.copy)

        def scores(n, parts=1):
            if not 0 <= n < STEPS:
                return
            for part in range(parts):
                scores_part(n, part, parts)

        def scores_part(n, part, parts):
            h, t = divmod(n, T)
            if part == 0:
                tiles["s_ps", n] = ps_scores.tile([P, S], F32, name="s_ps")
            keys = slice(part * S // parts, (part + 1) * S // parts)
            for u in range(PLANES):
                for e in range(2):
                    nc.tensor.matmul(
                        out=tiles["s_ps", n][:, keys],
                        lhsT=tiles["q_t", h][:, u, t * P : (t + 1) * P, e],
                        rhs=tiles["k_t", h][:, u, keys, e],
                        start=(u == 0 and e == 0),
                        stop=(u == PLANES - 1 and e == 1),
                    )

        def apply_mask(n):
            if not 0 <= n < STEPS:
                return
            masked = work.tile([P, S], F32, name="masked")
            nc.vector.scalar_tensor_tensor(
                out=masked[:],
                in0=tiles["s_ps", n][:],
                scalar=SCALE,
                in1=mask_sb[:, n % T, :],
                op0=ALU.mult,
                op1=ALU.mult,
            )
            tiles["masked", n] = masked

        def row_max(n):
            if not 0 <= n < STEPS:
                return
            neg_max = work.tile([P, 1], F32, name="neg_max")
            nc.vector.tensor_reduce(
                out=neg_max[:], in_=tiles["masked", n][:], axis=AXIS.X, op=ALU.max, negate=True
            )
            tiles["neg_max", n] = neg_max

        def exponential(n):
            if not 0 <= n < STEPS:
                return
            e_sb = work.tile([P, S], BF16, name="e_sb")
            h, t = divmod(n, T)
            if t == 0:
                tiles["row_sum", h] = work.tile([P, T], F32, name="row_sum")
            nc.scalar.activation(
                out=e_sb[:],
                in_=tiles["masked", n][:],
                func=ACT.Exp,
                bias=tiles["neg_max", n][:],
                scale=1.0,
                accum_out=tiles["row_sum", h][:, t : t + 1],
            )
            tiles["e_sb", n] = e_sb

        def reciprocal(n):
            if n % T or not 0 <= n < STEPS:
                return
            h = n // T
            inv_sum = work.tile([P, T], F32, name="inv_sum")
            nc.vector.reciprocal(out=inv_sum[:], in_=tiles["row_sum", h][:])
            tiles["inv_sum", h] = inv_sum

        def transpose_e(n):
            if n % 2 or not 0 <= n < STEPS:
                return
            et_ps = ps_et.tile([P, 2, PLANES * P], F32, name="et_ps")
            for i in range(2):
                transpose_words(nc, et_ps[:, i, :], tiles["e_sb", n + i], [0], ident_f32)
            e_grouped = work.tile([P, PAIR * PACK], BF16, name="e_grouped", align_bytes=64)
            nc.scalar.copy(
                out=e_grouped[:].bitcast(F32).rearrange("p (i r u) -> p i r u", i=2, u=PLANES),
                in_=et_ps[:].rearrange("p i (u r) -> p i r u", u=PLANES),
            )
            tiles["e_grouped", n] = e_grouped

        def quantise_e(n):
            if n % 2 or not 0 <= n < STEPS:
                return
            codes = work.tile([P, PAIR], U32, name="e_codes", align_bytes=64)
            scales = work.tile([P, PAIR], U8, name="e_scales", align_bytes=64)
            nc.vector.quantize_mx(
                out=codes[:].bitcast(FP8X4),
                scales=scales[:],
                in_=tiles["e_grouped", n][:],
            )
            tiles["e_codes", n] = codes
            tiles["e_scales", n] = scales

        def multiply_e_v(n):
            if not 0 <= n < STEPS:
                return
            h = n // T
            rows = slice(n % 2 * P, (n % 2 + 1) * P)
            o_ps = ps_mx.tile([P, V], F32, name="mx_bank")
            nc.tensor.matmul_mx(
                out=o_ps[:],
                lhsT=tiles["e_codes", n - n % 2][:, rows].bitcast(FP8X4),
                lhsT_scale=tiles["e_scales", n - n % 2][:, rows],
                rhs=tiles["v_codes", h][:].bitcast(FP8X4),
                rhs_scale=tiles["v_scales", h][:],
                start=True,
                stop=True,
            )
            tiles["o_ps", n] = o_ps

        def divide_and_store(n):
            if not 0 <= n < STEPS:
                return
            h, t = divmod(n, T)
            o_sb = work.tile([P, V], F32, name="o_sb")
            nc.scalar.activation(
                out=o_sb[:].rearrange("p (r c) -> p r c", c=T),
                in_=tiles["o_ps", n][:].rearrange("p (c r) -> p r c", c=T),
                func=ACT.Copy,
                scale=tiles["inv_sum", h][:, t : t + 1],
            )
            nc.sync.dma_start(out=out_rows[:, t, h * V : (h + 1) * V], in_=o_sb[:])

        bank = ps_mx.tile([P, PLANES * P], F32, name="mx_bank")
        transpose_rows("q_t", q_rows, 0, 0, 1, bank, nc.vector.tensor_copy)
        bank = ps_mx.tile([P, PLANES * P], F32, name="mx_bank")
        transpose_rows("k_t", k_rows, 0, 0, 1, bank, nc.scalar.copy)
        bank = ps_words.tile([P, PLANES * P], F32, name="word_bank")
        transpose_rows("k_t", k_rows, 0, 1, 2, bank, nc.vector.tensor_copy)
        bank = ps_words.tile([P, PLANES * P], F32, name="word_bank")
        transpose_rows("k_t", k_rows, 0, 2, 3, bank, nc.vector.tensor_copy)
        spread_bias(0)
        scores_part(0, 0, T)
        bank = ps_mx.tile([P, PLANES * P], F32, name="mx_bank")
        transpose_rows("k_t", k_rows, 0, 3, 4, bank, nc.vector.tensor_copy)
        scores_part(0, 1, T)
        bank = ps_words.tile([P, PLANES * PAIR], F32, name="word_bank")
        transpose_rows("q_t", q_rows, 0, 2, 4, bank, nc.vector.tensor_copy)
        bank = ps_words.tile([P, PLANES * P], F32, name="word_bank")
        transpose_rows("q_t", q_rows, 0, 1, 2, bank, nc.scalar.copy)
        scores_part(0, 2, T)
        scores_part(0, 3, T)
        transpose_value(1)
        transpose_value(0)
        scores(1)

        for step in range(STEPS - OUT):
            apply_mask(step)
            if step == 1:
                transpose_qk(T)
            if step >= 1:
                transpose_qk(step + QK)
            exponential(step + EXP)
            transpose_wv(step + WV_TRANSPOSE)
            project_v(step + PROJECT)
            transpose_e(step + E_TRANSPOSE)
            add_bias(step + BIAS)
            quantise_e(step + E_QUANTISE)
            multiply_e_v(step + EV)
            reciprocal(step + OUT)
            divide_and_store(step + OUT)
            row_max(step)
            if step == 6:
                spread_bias(1)
            scores(step + SCORES)
            quantise_v(step + V_QUANTISE)
            if step == 1:
                quantise_value()
            quantise_wv(step + WV_QUANTISE)
